import numpy as np
import ml_dtypes

BF16 = ml_dtypes.bfloat16


def bf(x):
    return np.asarray(x, np.float32).astype(BF16)


def f32(x):
    return np.asarray(x, np.float32)


def f64(x):
    return np.asarray(x).astype(np.float64)


def striped(idx):
    return np.tile(idx.reshape(-1, 16).T, (8, 1))


C, S, N, P = 128, 512, 256, 128
WB_SCALE = 0.3


def elu(a):
    return np.maximum(a, 0.0) + np.exp(np.minimum(a, 0.0)) - 1.0


def setup_inputs():
    return {"t": f32(np.random.standard_normal((C, S))), "wb": bf(WB_SCALE * np.random.standard_normal((C, C)) / np.sqrt(C)), "offs": striped(np.random.permutation(np.tile(np.arange(S), 2))[:N])}


def reference(t, wb, offs):
    idx = offs[:16].T.reshape(-1)
    z = elu(f64(t)[:, idx])
    u = f64(wb).T @ z[:, :P]
    return u * z[:, P:]

@@ -1,0 +1,50 @@
+import concourse.mybir as mybir
+
+F32 = mybir.dt.float32
+BF16 = mybir.dt.bfloat16
+U16 = mybir.dt.uint16
+ALU = mybir.AluOpType
+ACT = mybir.ActivationFunctionType
+
+C = 128
+S = 512
+N = 256
+P = 128
+
+FLOPS = 2 * C * C * P
+
+
+def tile_dmamodel_kernel(tc, t, wb, offs, out):
+    nc = tc.nc
+    with (
+        tc.tile_pool(name="held", bufs=1) as held,
+        tc.psum_pool(name="psum", bufs=1) as psum,
+    ):
+        offsets = held.tile([C, N // 16], U16, name="offsets")
+        nc.sync.dma_start(offsets[:], offs)
+        table = held.tile([C, S], F32, name="table")
+        nc.sync.dma_start(table[:], t)
+        weights = held.tile([C, C], BF16, name="weights")
+        nc.sync.dma_start(weights[:], wb)
+
+        v = held.tile([C, N], F32, name="v")
+        nc.scalar.activation(v[:], table[:].indirect(offsets[:]), ACT.Copy)
+
+        negative = held.tile([C, N], F32, name="negative")
+        nc.vector.tensor_scalar_min(negative[:], v[:], 0.0)
+        decay = held.tile([C, N], F32, name="decay")
+        nc.scalar.activation(decay[:], negative[:], ACT.Exp)
+        shifted = held.tile([C, N], F32, name="shifted")
+        nc.vector.tensor_scalar(shifted[:], v[:], 0.0, -1.0, ALU.max, ALU.add)
+
+        z_first = held.tile([C, P], BF16, name="z_first")
+        nc.vector.tensor_tensor(z_first[:], shifted[:, 0:P], decay[:, 0:P], ALU.add)
+        z_second = held.tile([C, P], F32, name="z_second")
+        nc.vector.tensor_tensor(z_second[:], shifted[:, P:N], decay[:, P:N], ALU.add)
+
+        u = psum.tile([C, P], F32, name="u")
+        nc.tensor.matmul(u[:], weights[:], z_first[:], start=True, stop=True)
+
+        product = held.tile([C, P], F32, name="product")
+        nc.vector.tensor_tensor(product[:], u[:], z_second[:], ALU.mult)
+        nc.sync.dma_start(out, product[:])

@@ -27,6 +27,10 @@ def tile_dmamodel_kernel(tc, t, wb, offs, out):
         weights = held.tile([C, C], BF16, name="weights")
         nc.sync.dma_start(weights[:], wb)
 
+        scratch = held.tile([C, 1], F32, name="scratch")
+        nc.vector.memset(scratch[:], 0.0)
+        nc.scalar.activation(scratch[:], scratch[:], ACT.Exp)
+
         v = held.tile([C, N], F32, name="v")
         nc.scalar.activation(v[:], table[:].indirect(offsets[:]), ACT.Copy)
 

@@ -10,6 +10,7 @@ C = 128
 S = 512
 N = 256
 P = 128
+W = P // 16
 
 FLOPS = 2 * C * C * P
 
@@ -31,23 +32,29 @@ def tile_dmamodel_kernel(tc, t, wb, offs, out):
         nc.vector.memset(scratch[:], 0.0)
         nc.scalar.activation(scratch[:], scratch[:], ACT.Exp)
 
-        v = held.tile([C, N], F32, name="v")
-        nc.scalar.activation(v[:], table[:].indirect(offsets[:]), ACT.Copy)
+        v = [held.tile([C, P], F32, name=f"v{k}") for k in range(2)]
+        for k in range(2):
+            piece = offsets[:, k * W : (k + 1) * W]
+            nc.scalar.activation(v[k][:], table[:].indirect(piece), ACT.Copy)
 
-        negative = held.tile([C, N], F32, name="negative")
-        nc.vector.tensor_scalar_min(negative[:], v[:], 0.0)
-        decay = held.tile([C, N], F32, name="decay")
-        nc.scalar.activation(decay[:], negative[:], ACT.Exp)
-        shifted = held.tile([C, N], F32, name="shifted")
-        nc.vector.tensor_scalar(shifted[:], v[:], 0.0, -1.0, ALU.max, ALU.add)
-
+        negative = [held.tile([C, P], F32, name=f"negative{k}") for k in range(2)]
+        decay = [held.tile([C, P], F32, name=f"decay{k}") for k in range(2)]
+        shifted = [held.tile([C, P], F32, name=f"shifted{k}") for k in range(2)]
         z_first = held.tile([C, P], BF16, name="z_first")
-        nc.vector.tensor_tensor(z_first[:], shifted[:, 0:P], decay[:, 0:P], ALU.add)
         z_second = held.tile([C, P], F32, name="z_second")
-        nc.vector.tensor_tensor(z_second[:], shifted[:, P:N], decay[:, P:N], ALU.add)
+
+        nc.vector.tensor_scalar_min(negative[0][:], v[0][:], 0.0)
+        nc.scalar.activation(decay[0][:], negative[0][:], ACT.Exp)
+        nc.vector.tensor_scalar(shifted[0][:], v[0][:], 0.0, -1.0, ALU.max, ALU.add)
+        nc.vector.tensor_scalar_min(negative[1][:], v[1][:], 0.0)
+        nc.scalar.activation(decay[1][:], negative[1][:], ACT.Exp)
+        nc.vector.tensor_tensor(z_first[:], shifted[0][:], decay[0][:], ALU.add)
 
         u = psum.tile([C, P], F32, name="u")
         nc.tensor.matmul(u[:], weights[:], z_first[:], start=True, stop=True)
+
+        nc.vector.tensor_scalar(shifted[1][:], v[1][:], 0.0, -1.0, ALU.max, ALU.add)
+        nc.vector.tensor_tensor(z_second[:], shifted[1][:], decay[1][:], ALU.add)
 
         product = held.tile([C, P], F32, name="product")
         nc.vector.tensor_tensor(product[:], u[:], z_second[:], ALU.mult)

@@ -33,29 +33,19 @@ def tile_dmamodel_kernel(tc, t, wb, offs, out):
         nc.scalar.activation(scratch[:], scratch[:], ACT.Exp)
 
         v = [held.tile([C, P], F32, name=f"v{k}") for k in range(2)]
+        grown = [held.tile([C, P], F32, name=f"grown{k}") for k in range(2)]
+        shifted = [held.tile([C, P], F32, name=f"shifted{k}") for k in range(2)]
+        z = [held.tile([C, P], (BF16, F32)[k], name=f"z{k}") for k in range(2)]
         for k in range(2):
             piece = offsets[:, k * W : (k + 1) * W]
             nc.scalar.activation(v[k][:], table[:].indirect(piece), ACT.Copy)
-
-        negative = [held.tile([C, P], F32, name=f"negative{k}") for k in range(2)]
-        decay = [held.tile([C, P], F32, name=f"decay{k}") for k in range(2)]
-        shifted = [held.tile([C, P], F32, name=f"shifted{k}") for k in range(2)]
-        z_first = held.tile([C, P], BF16, name="z_first")
-        z_second = held.tile([C, P], F32, name="z_second")
-
-        nc.vector.tensor_scalar_min(negative[0][:], v[0][:], 0.0)
-        nc.scalar.activation(decay[0][:], negative[0][:], ACT.Exp)
-        nc.vector.tensor_scalar(shifted[0][:], v[0][:], 0.0, -1.0, ALU.max, ALU.add)
-        nc.vector.tensor_scalar_min(negative[1][:], v[1][:], 0.0)
-        nc.scalar.activation(decay[1][:], negative[1][:], ACT.Exp)
-        nc.vector.tensor_tensor(z_first[:], shifted[0][:], decay[0][:], ALU.add)
+            nc.scalar.activation(grown[k][:], v[k][:], ACT.Exp)
+            nc.vector.tensor_scalar(shifted[k][:], v[k][:], 0.0, -1.0, ALU.max, ALU.add)
+            nc.vector.scalar_tensor_tensor(z[k][:], grown[k][:], 1.0, shifted[k][:], ALU.min, ALU.add)
 
         u = psum.tile([C, P], F32, name="u")
-        nc.tensor.matmul(u[:], weights[:], z_first[:], start=True, stop=True)
-
-        nc.vector.tensor_scalar(shifted[1][:], v[1][:], 0.0, -1.0, ALU.max, ALU.add)
-        nc.vector.tensor_tensor(z_second[:], shifted[1][:], decay[1][:], ALU.add)
+        nc.tensor.matmul(u[:], weights[:], z[0][:], start=True, stop=True)
 
         product = held.tile([C, P], F32, name="product")
-        nc.vector.tensor_tensor(product[:], u[:], z_second[:], ALU.mult)
+        nc.vector.tensor_tensor(product[:], u[:], z[1][:], ALU.mult)
         nc.sync.dma_start(out, product[:])

@@ -6,13 +6,13 @@ U16 = mybir.dt.uint16
 ALU = mybir.AluOpType
 ACT = mybir.ActivationFunctionType
 
-C = 128
-S = 512
-N = 256
-P = 128
-W = P // 16
+FEATURES = 128
+NODES = 512
+PAIRS = 128
+ENTRIES = 2 * PAIRS
+ENTRIES_A_COLUMN = 16
 
-FLOPS = 2 * C * C * P
+FLOPS = 2 * FEATURES * FEATURES * PAIRS
 
 
 def tile_dmamodel_kernel(tc, t, wb, offs, out):
@@ -21,31 +21,34 @@ def tile_dmamodel_kernel(tc, t, wb, offs, out):
         tc.tile_pool(name="held", bufs=1) as held,
         tc.psum_pool(name="psum", bufs=1) as psum,
     ):
-        offsets = held.tile([C, N // 16], U16, name="offsets")
+        table = held.tile([FEATURES, NODES], F32, name="table")
+        nc.scalar.dma_start(table[:], t)
+        offsets = held.tile([FEATURES, ENTRIES // ENTRIES_A_COLUMN], U16, name="offsets")
         nc.sync.dma_start(offsets[:], offs)
-        table = held.tile([C, S], F32, name="table")
-        nc.sync.dma_start(table[:], t)
-        weights = held.tile([C, C], BF16, name="weights")
+        weights = held.tile([FEATURES, FEATURES], BF16, name="weights")
         nc.sync.dma_start(weights[:], wb)
 
-        scratch = held.tile([C, 1], F32, name="scratch")
+        scratch = held.tile([FEATURES, 1], F32, name="scratch")
         nc.vector.memset(scratch[:], 0.0)
         nc.scalar.activation(scratch[:], scratch[:], ACT.Exp)
 
-        v = [held.tile([C, P], F32, name=f"v{k}") for k in range(2)]
-        grown = [held.tile([C, P], F32, name=f"grown{k}") for k in range(2)]
-        shifted = [held.tile([C, P], F32, name=f"shifted{k}") for k in range(2)]
-        z = [held.tile([C, P], (BF16, F32)[k], name=f"z{k}") for k in range(2)]
-        for k in range(2):
-            piece = offsets[:, k * W : (k + 1) * W]
-            nc.scalar.activation(v[k][:], table[:].indirect(piece), ACT.Copy)
-            nc.scalar.activation(grown[k][:], v[k][:], ACT.Exp)
-            nc.vector.tensor_scalar(shifted[k][:], v[k][:], 0.0, -1.0, ALU.max, ALU.add)
-            nc.vector.scalar_tensor_tensor(z[k][:], grown[k][:], 1.0, shifted[k][:], ALU.min, ALU.add)
+        z_first = held.tile([FEATURES, PAIRS], BF16, name="z_first")
+        z_second = held.tile([FEATURES, PAIRS], F32, name="z_second")
+        columns = PAIRS // ENTRIES_A_COLUMN
+        for side, z in enumerate((z_first, z_second)):
+            v = held.tile([FEATURES, PAIRS], F32, name=f"v{side}")
+            piece = offsets[:, side * columns : (side + 1) * columns]
+            nc.scalar.activation(v[:], table[:].indirect(piece), ACT.Copy)
 
-        u = psum.tile([C, P], F32, name="u")
-        nc.tensor.matmul(u[:], weights[:], z[0][:], start=True, stop=True)
+            grown = held.tile([FEATURES, PAIRS], F32, name=f"grown{side}")
+            nc.scalar.activation(grown[:], v[:], ACT.Exp)
+            shifted = held.tile([FEATURES, PAIRS], F32, name=f"shifted{side}")
+            nc.vector.tensor_scalar(shifted[:], v[:], 0.0, -1.0, ALU.max, ALU.add)
+            nc.vector.scalar_tensor_tensor(z[:], grown[:], 1.0, shifted[:], ALU.min, ALU.add)
 
-        product = held.tile([C, P], F32, name="product")
-        nc.vector.tensor_tensor(product[:], u[:], z[1][:], ALU.mult)
+        u = psum.tile([FEATURES, PAIRS], F32, name="u")
+        nc.tensor.matmul(u[:], weights[:], z_first[:], start=True, stop=True)
+
+        product = held.tile([FEATURES, PAIRS], F32, name="product")
+        nc.vector.tensor_tensor(product[:], u[:], z_second[:], ALU.mult)
         nc.sync.dma_start(out, product[:])

@@ -22,7 +22,9 @@ def tile_dmamodel_kernel(tc, t, wb, offs, out):
         tc.psum_pool(name="psum", bufs=1) as psum,
     ):
         table = held.tile([FEATURES, NODES], F32, name="table")
-        nc.scalar.dma_start(table[:], t)
+        half = NODES // 2
+        nc.sync.dma_start(table[:, :half], t[:, :half])
+        nc.scalar.dma_start(table[:, half:], t[:, half:])
         offsets = held.tile([FEATURES, ENTRIES // ENTRIES_A_COLUMN], U16, name="offsets")
         nc.sync.dma_start(offsets[:], offs)
         weights = held.tile([FEATURES, FEATURES], BF16, name="weights")

@@ -22,9 +22,8 @@ def tile_dmamodel_kernel(tc, t, wb, offs, out):
         tc.psum_pool(name="psum", bufs=1) as psum,
     ):
         table = held.tile([FEATURES, NODES], F32, name="table")
-        half = NODES // 2
-        nc.sync.dma_start(table[:, :half], t[:, :half])
-        nc.scalar.dma_start(table[:, half:], t[:, half:])
+        nc.sync.dma_start(table[0::2, :], t[0::2, :])
+        nc.scalar.dma_start(table[1::2, :], t[1::2, :])
         offsets = held.tile([FEATURES, ENTRIES // ENTRIES_A_COLUMN], U16, name="offsets")
         nc.sync.dma_start(offsets[:], offs)
         weights = held.tile([FEATURES, FEATURES], BF16, name="weights")

@@ -33,22 +33,34 @@ def tile_dmamodel_kernel(tc, t, wb, offs, out):
         nc.vector.memset(scratch[:], 0.0)
         nc.scalar.activation(scratch[:], scratch[:], ACT.Exp)
 
-        z_first = held.tile([FEATURES, PAIRS], BF16, name="z_first")
-        z_second = held.tile([FEATURES, PAIRS], F32, name="z_second")
         columns = PAIRS // ENTRIES_A_COLUMN
-        for side, z in enumerate((z_first, z_second)):
-            v = held.tile([FEATURES, PAIRS], F32, name=f"v{side}")
-            piece = offsets[:, side * columns : (side + 1) * columns]
-            nc.scalar.activation(v[:], table[:].indirect(piece), ACT.Copy)
-
-            grown = held.tile([FEATURES, PAIRS], F32, name=f"grown{side}")
-            nc.scalar.activation(grown[:], v[:], ACT.Exp)
-            shifted = held.tile([FEATURES, PAIRS], F32, name=f"shifted{side}")
-            nc.vector.tensor_scalar(shifted[:], v[:], 0.0, -1.0, ALU.max, ALU.add)
-            nc.vector.scalar_tensor_tensor(z[:], grown[:], 1.0, shifted[:], ALU.min, ALU.add)
-
+        v_first = held.tile([FEATURES, PAIRS], F32, name="v_first")
+        nc.scalar.activation(v_first[:], table[:].indirect(offsets[:, :columns]), ACT.Copy)
         u = psum.tile([FEATURES, PAIRS], F32, name="u")
-        nc.tensor.matmul(u[:], weights[:], z_first[:], start=True, stop=True)
+        positive = held.tile([FEATURES, PAIRS], BF16, name="positive")
+        nc.vector.tensor_scalar(positive[:], v_first[:], 0.0, None, ALU.max)
+        nc.tensor.matmul(u[:], weights[:], positive[:], start=True, stop=False)
+        grown_first = held.tile([FEATURES, PAIRS], F32, name="grown_first")
+        nc.scalar.activation(grown_first[:], v_first[:], ACT.Exp)
+        negative = held.tile([FEATURES, PAIRS], BF16, name="negative")
+        nc.vector.tensor_scalar(negative[:], grown_first[:], 1.0, -1.0, ALU.min, ALU.add)
+        nc.tensor.matmul(u[:], weights[:], negative[:], start=False, stop=True)
+
+        z_second = held.tile([FEATURES, PAIRS], F32, name="z_second")
+        group = PAIRS // 2
+        for g in range(2):
+            pairs = slice(g * group, (g + 1) * group)
+            start = (PAIRS + g * group) // ENTRIES_A_COLUMN
+            piece = offsets[:, start : start + group // ENTRIES_A_COLUMN]
+            v = held.tile([FEATURES, group], F32, name=f"v_second{g}")
+            nc.scalar.activation(v[:], table[:].indirect(piece), ACT.Copy)
+            grown = held.tile([FEATURES, group], F32, name=f"grown_second{g}")
+            nc.scalar.activation(grown[:], v[:], ACT.Exp)
+            shifted = held.tile([FEATURES, group], F32, name=f"shifted{g}")
+            nc.vector.tensor_scalar(shifted[:], v[:], 0.0, -1.0, ALU.max, ALU.add)
+            nc.vector.scalar_tensor_tensor(
+                z_second[:, pairs], grown[:], 1.0, shifted[:], ALU.min, ALU.add
+            )
 
         product = held.tile([FEATURES, PAIRS], F32, name="product")
         nc.vector.tensor_tensor(product[:], u[:], z_second[:], ALU.mult)

import concourse.mybir as mybir

F32 = mybir.dt.float32
BF16 = mybir.dt.bfloat16
U16 = mybir.dt.uint16
ALU = mybir.AluOpType
ACT = mybir.ActivationFunctionType

FEATURES = 128
NODES = 512
PAIRS = 128
ENTRIES = 2 * PAIRS
ENTRIES_A_COLUMN = 16

FLOPS = 2 * FEATURES * FEATURES * PAIRS


def tile_dmamodel_kernel(tc, t, wb, offs, out):
    nc = tc.nc
    with (
        tc.tile_pool(name="held", bufs=1) as held,
        tc.psum_pool(name="psum", bufs=1) as psum,
    ):
        table = held.tile([FEATURES, NODES], F32, name="table")
        nc.sync.dma_start(table[0::2, :], t[0::2, :])
        nc.scalar.dma_start(table[1::2, :], t[1::2, :])
        offsets = held.tile([FEATURES, ENTRIES // ENTRIES_A_COLUMN], U16, name="offsets")
        nc.sync.dma_start(offsets[:], offs)
        weights = held.tile([FEATURES, FEATURES], BF16, name="weights")
        nc.sync.dma_start(weights[:], wb)

        scratch = held.tile([FEATURES, 1], F32, name="scratch")
        nc.vector.memset(scratch[:], 0.0)
        nc.scalar.activation(scratch[:], scratch[:], ACT.Exp)

        columns = PAIRS // ENTRIES_A_COLUMN
        v_first = held.tile([FEATURES, PAIRS], F32, name="v_first")
        nc.scalar.activation(v_first[:], table[:].indirect(offsets[:, :columns]), ACT.Copy)
        u = psum.tile([FEATURES, PAIRS], F32, name="u")
        positive = held.tile([FEATURES, PAIRS], BF16, name="positive")
        nc.vector.tensor_scalar(positive[:], v_first[:], 0.0, None, ALU.max)
        nc.tensor.matmul(u[:], weights[:], positive[:], start=True, stop=False)
        grown_first = held.tile([FEATURES, PAIRS], F32, name="grown_first")
        nc.scalar.activation(grown_first[:], v_first[:], ACT.Exp)
        negative = held.tile([FEATURES, PAIRS], BF16, name="negative")
        nc.vector.tensor_scalar(negative[:], grown_first[:], 1.0, -1.0, ALU.min, ALU.add)
        nc.tensor.matmul(u[:], weights[:], negative[:], start=False, stop=True)

        z_second = held.tile([FEATURES, PAIRS], F32, name="z_second")
        group = PAIRS // 2
        for g in range(2):
            pairs = slice(g * group, (g + 1) * group)
            start = (PAIRS + g * group) // ENTRIES_A_COLUMN
            piece = offsets[:, start : start + group // ENTRIES_A_COLUMN]
            v = held.tile([FEATURES, group], F32, name=f"v_second{g}")
            nc.scalar.activation(v[:], table[:].indirect(piece), ACT.Copy)
            grown = held.tile([FEATURES, group], F32, name=f"grown_second{g}")
            nc.scalar.activation(grown[:], v[:], ACT.Exp)
            shifted = held.tile([FEATURES, group], F32, name=f"shifted{g}")
            nc.vector.tensor_scalar(shifted[:], v[:], 0.0, -1.0, ALU.max, ALU.add)
            nc.vector.scalar_tensor_tensor(
                z_second[:, pairs], grown[:], 1.0, shifted[:], ALU.min, ALU.add
            )

        product = held.tile([FEATURES, PAIRS], F32, name="product")
        nc.vector.tensor_tensor(product[:], u[:], z_second[:], ALU.mult)
        nc.sync.dma_start(out, product[:])
